import numpy as np
import ml_dtypes


def mxq(x, axis, fmt="e4m3"):
    dtype, down = {"e4m3": (ml_dtypes.float8_e4m3fn, 7), "e5m2": (ml_dtypes.float8_e5m2, 14)}[fmt]
    v = np.moveaxis(np.asarray(x, np.float32).astype(ml_dtypes.bfloat16).astype(np.float64), axis, -1)
    blocks = v.reshape(v.shape[:-1] + (-1, 32))
    amax = np.abs(blocks).max(-1, keepdims=True)
    byte = np.maximum(np.where(amax > 0, np.frexp(amax)[1] - 1 + 127, 0) - down, 1)
    scale = np.exp2(byte - 127.0)
    codes = (blocks / scale).astype(np.float32).astype(dtype).astype(np.float64)
    return np.moveaxis((codes * scale).reshape(v.shape), -1, axis)


WIDE = False


def mx_kscale(k):
    if not WIDE:
        return np.ones(k)
    levels = np.array([10, -10, 5, -5, 0])
    a = np.random.permutation(np.resize(levels, k // 512 * 4)).reshape(k // 512, 4)
    idx = np.arange(k)
    return np.exp2(a[idx // 512, idx % 128 // 32])


BF16 = ml_dtypes.bfloat16


def bf(x):
    return np.asarray(x, np.float32).astype(BF16)


def f64(x):
    return np.asarray(x).astype(np.float64)


B, L, D = 3, 512, 512
SIG = 2.0


def setup_inputs():
    s, t = mx_kscale(D), mx_kscale(D)
    return {"x1": bf(np.random.standard_normal((B, L, D)) * s),
            "bi_linear_w": bf(np.random.standard_normal((D, D)) * SIG / D / s[:, None] * t),
            "x2": bf(np.random.standard_normal((B, L, D)) / t)}


def reference(x1, bi_linear_w, x2):
    h = mxq(f64(x1), 2, "e4m3") @ mxq(f64(bi_linear_w), 0, "e4m3")
    return mxq(h, 2, "e4m3") @ mxq(f64(x2), 2, "e4m3").transpose(0, 2, 1)

@@ -1,0 +1,166 @@
+from contextlib import ExitStack
+
+import concourse.mybir as mybir
+from concourse.masks import make_identity
+
+F32 = mybir.dt.float32
+BF16 = mybir.dt.bfloat16
+U32 = mybir.dt.uint32
+U8 = mybir.dt.uint8
+FP8X4 = mybir.dt.float8_e4m3fn_x4
+
+P = 128
+B, L, D = 3, 512, 512
+FLOPS = 2 * 2 * B * L * D * D
+
+PINNED = False
+LOADS = [["w",0],["x1",0],["x2",0],["x1",1],["x2",1],["x1",2],["x2",2]]
+STEPS = [["rw",0,"v"],["rw",3,"s"],["rw",1,"v"],["qw",0,256],["rw",2,"v"],["qw",256,512],["t","x1",0,0],["t","x1",0,1],["c","x1",0,0,"s"],["c","x1",0,1,"v"],["q","x1",0,0,256],["q","x1",0,256,512],["t","x2",0,0],["t","x2",0,1],["c","x2",0,0,"s"],["c","x2",0,1,"v"],["q","x2",0,0,512],["s1",0,0],["s1",0,1],["s1",0,2],["s1",0,3],["ch",0,0,"s"],["ch",0,1,"s"],["q","h",0,0,256],["ch",0,2,"v"],["ch",0,3,"s"],["q","h",0,256,512],["t","x1",1,0],["t","x1",1,1],["c","x1",1,0,"s"],["c","x1",1,1,"v"],["q","x1",1,0,256],["q","x1",1,256,512],["s2",0,0],["s2",0,1],["s2",0,2],["s2",0,3],["co",0,0,"s"],["co",0,1,"s"],["st",0,0,2],["co",0,2,"s"],["co",0,3,"v"],["st",0,2,4],["s1",1,0],["s1",1,1],["s1",1,2],["s1",1,3],["ch",1,0,"s"],["ch",1,1,"s"],["q","h",1,0,256],["ch",1,2,"v"],["ch",1,3,"s"],["q","h",1,256,512],["t","x2",1,0],["t","x2",1,1],["c","x2",1,0,"s"],["c","x2",1,1,"v"],["q","x2",1,0,512],["t","x1",2,0],["t","x1",2,1],["c","x1",2,0,"s"],["c","x1",2,1,"v"],["q","x1",2,0,256],["q","x1",2,256,512],["s2",1,0],["s2",1,1],["s2",1,2],["s2",1,3],["co",1,0,"s"],["co",1,1,"s"],["st",1,0,2],["co",1,2,"s"],["co",1,3,"v"],["st",1,2,4],["s1",2,0],["s1",2,1],["s1",2,2],["s1",2,3],["ch",2,0,"s"],["ch",2,1,"s"],["q","h",2,0,256],["ch",2,2,"v"],["ch",2,3,"s"],["q","h",2,256,512],["t","x2",2,0],["t","x2",2,1],["c","x2",2,0,"s"],["c","x2",2,1,"v"],["q","x2",2,0,512],["s2",2,0],["s2",2,1],["s2",2,2],["s2",2,3],["co",2,0,"s"],["st",2,0,1],["co",2,1,"v"],["st",2,1,2],["co",2,2,"s"],["st",2,2,3],["co",2,3,"v"],["st",2,3,4]]
+
+
+def tile_coattentionandcombine_pa_kernel(tc, x1, bi_linear_w, x2, out):
+    nc = tc.nc
+    with ExitStack() as ctx:
+        keep = ctx.enter_context(tc.tile_pool(name="keep", bufs=1))
+        psum = ctx.enter_context(tc.psum_pool(name="psum", bufs=8))
+        if PINNED:
+            ctx.enter_context(tc.manual_schedule())
+
+        def copy(eng, dst, src):
+            if eng == "v":
+                nc.vector.tensor_copy(out=dst, in_=src)
+            else:
+                nc.scalar.copy(out=dst, in_=src)
+
+        w_sb = keep.tile([P, 4 * D], BF16, name="w_sb")
+        w_grp = keep.tile([P, 4 * D], BF16, name="w_grp", align_bytes=64)
+        w_codes = keep.tile([P, D], U32, name="w_codes", align_bytes=64)
+        w_scales = keep.tile([P, D], U8, name="w_scales", align_bytes=64)
+        ident = keep.tile([P, P], F32, name="ident")
+        raw = {}
+        grp = {}
+        codes = {}
+        scales = {}
+        for b in range(B):
+            for s in ("x1", "x2", "h"):
+                if s != "h":
+                    raw[(s, b)] = keep.tile([P, 4 * D], BF16, name="%s_raw%d" % (s, b))
+                grp[(s, b)] = keep.tile([P, 4 * L], BF16, name="%s_grp%d" % (s, b), align_bytes=64)
+                codes[(s, b)] = keep.tile([P, L], U32, name="%s_codes%d" % (s, b), align_bytes=64)
+                scales[(s, b)] = keep.tile([P, L], U8, name="%s_scales%d" % (s, b), align_bytes=64)
+        out_sb = [keep.tile([P, 4 * L], F32, name="out_sb%d" % b) for b in range(B)]
+
+        for s, b in LOADS:
+            if s == "w":
+                nc.sync.dma_start(
+                    out=w_sb[:].rearrange("p (u r) -> p u r", u=2),
+                    in_=bi_linear_w.rearrange("(u p e) c -> p u (e c)", u=2, e=2),
+                )
+            elif s == "x1":
+                nc.sync.dma_start(out=raw[(s, b)][:], in_=x1[b].rearrange("(q i) d -> q (i d)", i=4))
+            else:
+                nc.sync.dma_start(
+                    out=raw[(s, b)][:].rearrange("p (h r) -> p h r", h=2),
+                    in_=x2[b].rearrange("(h q i) d -> q h (i d)", h=2, i=2),
+                )
+        make_identity(nc, ident[:])
+
+        banks = {}
+
+        def quantise(s, b, lo, hi):
+            nc.vector.quantize_mx(
+                out=codes[(s, b)][:, lo:hi].bitcast(FP8X4),
+                scales=scales[(s, b)][:, lo:hi],
+                in_=grp[(s, b)][:, 4 * lo : 4 * hi],
+            )
+
+        for step in STEPS:
+            kind = step[0]
+            if kind == "rw":
+                t, eng = step[1], step[2]
+                u, e = t // 2, t % 2
+                src = w_sb[:].rearrange("p (t u m e) -> p t u m e", t=4, u=2, e=2)[:, :, u, :, e]
+                copy(
+                    eng,
+                    w_grp[:, t * 512 : (t + 1) * 512].rearrange("p (m t) -> p m t", t=4),
+                    src.rearrange("p t m -> p m t"),
+                )
+            elif kind == "qw":
+                lo, hi = step[1], step[2]
+                nc.vector.quantize_mx(
+                    out=w_codes[:, lo:hi].bitcast(FP8X4),
+                    scales=w_scales[:, lo:hi],
+                    in_=w_grp[:, 4 * lo : 4 * hi],
+                )
+            elif kind == "t":
+                s, b, g = step[1], step[2], step[3]
+                words = raw[(s, b)][:].bitcast(F32)
+                bank = psum.tile([P, 512], F32, tag="bank", name="t_%s%d%d" % (s, b, g))
+                for a in range(4):
+                    nc.tensor.transpose(
+                        bank[:, a * P : (a + 1) * P],
+                        words[:, g * 512 + a * P : g * 512 + (a + 1) * P],
+                        ident[:],
+                    )
+                banks[("t", s, b, g)] = bank
+            elif kind == "c":
+                s, b, g, eng = step[1], step[2], step[3], step[4]
+                bank = banks[("t", s, b, g)]
+                dst = grp[(s, b)][:].bitcast(F32)[:, g * 512 : (g + 1) * 512]
+                if s == "x1":
+                    copy(
+                        eng,
+                        dst.rearrange("p (i q u) -> p i q u", i=2, u=2),
+                        bank[:].rearrange("p (i u q) -> p i q u", i=2, u=2),
+                    )
+                else:
+                    copy(
+                        eng,
+                        dst.rearrange("p (q a) -> p q a", a=4),
+                        bank[:].rearrange("p (a q) -> p q a", a=4),
+                    )
+            elif kind == "q":
+                quantise(step[1], step[2], step[3], step[4])
+            elif kind == "s1":
+                b, i = step[1], step[2]
+                bank = psum.tile([P, 512], F32, tag="bank", name="h_%d%d" % (b, i))
+                for t in range(4):
+                    nc.tensor.matmul_mx(
+                        out=bank[:, t * P : (t + 1) * P],
+                        lhsT=w_codes[:, t * P : (t + 1) * P].bitcast(FP8X4),
+                        lhsT_scale=w_scales[:, t * P : (t + 1) * P],
+                        rhs=codes[("x1", b)][:, i * P : (i + 1) * P].bitcast(FP8X4),
+                        rhs_scale=scales[("x1", b)][:, i * P : (i + 1) * P],
+                        start=True,
+                        stop=True,
+                    )
+                banks[("h", b, i)] = bank
+            elif kind == "ch":
+                b, i, eng = step[1], step[2], step[3]
+                copy(
+                    eng,
+                    grp[("h", b)][:, i * 512 : (i + 1) * 512].rearrange("p (q t) -> p q t", t=4),
+                    banks[("h", b, i)][:].rearrange("p (t q) -> p q t", t=4),
+                )
+            elif kind == "s2":
+                b, i = step[1], step[2]
+                bank = psum.tile([P, 512], F32, tag="bank", name="o_%d%d" % (b, i))
+                nc.tensor.matmul_mx(
+                    out=bank[:],
+                    lhsT=codes[("h", b)][:, i * P : (i + 1) * P].bitcast(FP8X4),
+                    lhsT_scale=scales[("h", b)][:, i * P : (i + 1) * P],
+                    rhs=codes[("x2", b)][:].bitcast(FP8X4),
+                    rhs_scale=scales[("x2", b)][:],
+                    start=True,
+                    stop=True,
+                )
+                banks[("o", b, i)] = bank
+            elif kind == "co":
+                b, i, eng = step[1], step[2], step[3]
+                copy(eng, out_sb[b][:, i * 512 : (i + 1) * 512], banks[("o", b, i)][:])
+            elif kind == "st":
+                b, lo, hi = step[1], step[2], step[3]
+                nc.sync.dma_start(
+                    out=out[b].rearrange("(q i) m -> q (i m)", i=4)[:, lo * 512 : hi * 512],
+                    in_=out_sb[b][:, lo * 512 : hi * 512],
+                )

@@ -13,9 +13,9 @@ P = 128
 B, L, D = 3, 512, 512
 FLOPS = 2 * 2 * B * L * D * D
 
-PINNED = False
-LOADS = [["w",0],["x1",0],["x2",0],["x1",1],["x2",1],["x1",2],["x2",2]]
-STEPS = [["rw",0,"v"],["rw",3,"s"],["rw",1,"v"],["qw",0,256],["rw",2,"v"],["qw",256,512],["t","x1",0,0],["t","x1",0,1],["c","x1",0,0,"s"],["c","x1",0,1,"v"],["q","x1",0,0,256],["q","x1",0,256,512],["t","x2",0,0],["t","x2",0,1],["c","x2",0,0,"s"],["c","x2",0,1,"v"],["q","x2",0,0,512],["s1",0,0],["s1",0,1],["s1",0,2],["s1",0,3],["ch",0,0,"s"],["ch",0,1,"s"],["q","h",0,0,256],["ch",0,2,"v"],["ch",0,3,"s"],["q","h",0,256,512],["t","x1",1,0],["t","x1",1,1],["c","x1",1,0,"s"],["c","x1",1,1,"v"],["q","x1",1,0,256],["q","x1",1,256,512],["s2",0,0],["s2",0,1],["s2",0,2],["s2",0,3],["co",0,0,"s"],["co",0,1,"s"],["st",0,0,2],["co",0,2,"s"],["co",0,3,"v"],["st",0,2,4],["s1",1,0],["s1",1,1],["s1",1,2],["s1",1,3],["ch",1,0,"s"],["ch",1,1,"s"],["q","h",1,0,256],["ch",1,2,"v"],["ch",1,3,"s"],["q","h",1,256,512],["t","x2",1,0],["t","x2",1,1],["c","x2",1,0,"s"],["c","x2",1,1,"v"],["q","x2",1,0,512],["t","x1",2,0],["t","x1",2,1],["c","x1",2,0,"s"],["c","x1",2,1,"v"],["q","x1",2,0,256],["q","x1",2,256,512],["s2",1,0],["s2",1,1],["s2",1,2],["s2",1,3],["co",1,0,"s"],["co",1,1,"s"],["st",1,0,2],["co",1,2,"s"],["co",1,3,"v"],["st",1,2,4],["s1",2,0],["s1",2,1],["s1",2,2],["s1",2,3],["ch",2,0,"s"],["ch",2,1,"s"],["q","h",2,0,256],["ch",2,2,"v"],["ch",2,3,"s"],["q","h",2,256,512],["t","x2",2,0],["t","x2",2,1],["c","x2",2,0,"s"],["c","x2",2,1,"v"],["q","x2",2,0,512],["s2",2,0],["s2",2,1],["s2",2,2],["s2",2,3],["co",2,0,"s"],["st",2,0,1],["co",2,1,"v"],["st",2,1,2],["co",2,2,"s"],["st",2,2,3],["co",2,3,"v"],["st",2,3,4]]
+PINNED = True
+LOADS = [["w",0,-1],["x1",0,-1],["x2",0,-1],["x1",1,-1],["x2",1,-1],["x1",2,-1],["x2",2,-1]]
+STEPS = [["rw",1,"v"],["rw",3,"v"],["t","x1",0,0],["t","x1",0,1],["rw",0,"v"],["t","x2",0,0],["qw",0,256],["c","x1",0,0,"v"],["rw",2,"s"],["c","x1",0,1,"s"],["qw",256,512],["q","x1",0,0,256],["t","x2",0,1],["q","x1",0,256,512],["s1",0,1],["s1",0,2],["s1",0,0],["c","x2",0,1,"s"],["s1",0,3],["c","x2",0,0,"v"],["q","x2",0,0,512],["t","x1",1,0],["t","x2",1,1],["ch",0,1,"s"],["ch",0,0,"s"],["t","x2",1,0],["c","x1",1,0,"s"],["ch",0,2,"v"],["ch",0,3,"v"],["t","x1",1,1],["q","h",0,256,512],["c","x2",1,1,"s"],["s2",0,3],["q","x1",1,0,256],["c","x2",1,0,"s"],["q","h",0,0,256],["c","x1",1,1,"v"],["s1",1,0],["q","x2",1,0,512],["s1",1,1],["co",0,3,"s"],["s2",0,2],["ch",1,1,"v"],["ch",1,0,"s"],["co",0,2,"s"],["t","x1",2,1],["q","x1",1,256,512],["c","x1",2,1,"s"],["q","h",1,0,256],["t","x1",2,0],["s2",0,0],["s2",0,1],["c","x1",2,0,"v"],["q","x1",2,256,512],["q","x1",2,0,256],["s1",1,2],["co",0,0,"s"],["s1",1,3],["s2",1,1],["ch",1,2,"v"],["st",0,2,4],["t","x2",2,1],["c","x2",2,1,"v"],["co",0,1,"s"],["ch",1,3,"s"],["t","x2",2,0],["s2",1,0],["q","h",1,256,512],["s1",2,2],["c","x2",2,0,"v"],["s1",2,3],["s2",1,3],["ch",2,3,"v"],["co",1,1,"s"],["s2",1,2],["co",1,0,"s"],["s1",2,1],["q","x2",2,0,512],["ch",2,2,"s"],["co",1,3,"s"],["st",0,0,2],["s1",2,0],["q","h",2,256,512],["ch",2,0,"v"],["s2",2,3],["co",1,2,"s"],["ch",2,1,"s"],["co",2,3,"s"],["q","h",2,0,256],["s2",2,2],["st",1,0,2],["st",1,2,4],["st",2,3,4],["s2",2,1],["co",2,2,"v"],["st",2,2,3],["co",2,1,"s"],["st",2,1,2],["s2",2,0],["co",2,0,"s"],["st",2,0,1]]
 
 
 def tile_coattentionandcombine_pa_kernel(tc, x1, bi_linear_w, x2, out):
@@ -50,14 +50,24 @@ def tile_coattentionandcombine_pa_kernel(tc, x1, bi_linear_w, x2, out):
                 scales[(s, b)] = keep.tile([P, L], U8, name="%s_scales%d" % (s, b), align_bytes=64)
         out_sb = [keep.tile([P, 4 * L], F32, name="out_sb%d" % b) for b in range(B)]
 
-        for s, b in LOADS:
+        for s, b, g in LOADS:
             if s == "w":
                 nc.sync.dma_start(
                     out=w_sb[:].rearrange("p (u r) -> p u r", u=2),
                     in_=bi_linear_w.rearrange("(u p e) c -> p u (e c)", u=2, e=2),
                 )
-            elif s == "x1":
+            elif s == "x1" and g < 0:
                 nc.sync.dma_start(out=raw[(s, b)][:], in_=x1[b].rearrange("(q i) d -> q (i d)", i=4))
+            elif s == "x1":
+                nc.sync.dma_start(
+                    out=raw[(s, b)][:, g * 1024 : (g + 1) * 1024],
+                    in_=x1[b].rearrange("(q i) d -> q (i d)", i=4)[:, g * 1024 : (g + 1) * 1024],
+                )
+            elif g >= 0:
+                nc.sync.dma_start(
+                    out=raw[(s, b)][:, g * 1024 : (g + 1) * 1024],
+                    in_=x2[b, g * 256 : (g + 1) * 256, :].rearrange("(q i) d -> q (i d)", i=2),
+                )
             else:
                 nc.sync.dma_start(
                     out=raw[(s, b)][:].rearrange("p (h r) -> p h r", h=2),

@@ -7,6 +7,7 @@ F32 = mybir.dt.float32
 BF16 = mybir.dt.bfloat16
 U32 = mybir.dt.uint32
 U8 = mybir.dt.uint8
+I32 = mybir.dt.int32
 FP8X4 = mybir.dt.float8_e4m3fn_x4
 
 P = 128
@@ -15,7 +16,7 @@ FLOPS = 2 * 2 * B * L * D * D
 
 PINNED = True
 LOADS = [["w",0,-1],["x1",0,-1],["x2",0,-1],["x1",1,-1],["x2",1,-1],["x1",2,-1],["x2",2,-1]]
-STEPS = [["rw",1,"v"],["rw",3,"v"],["t","x1",0,0],["t","x1",0,1],["rw",0,"v"],["t","x2",0,0],["qw",0,256],["c","x1",0,0,"v"],["rw",2,"s"],["c","x1",0,1,"s"],["qw",256,512],["q","x1",0,0,256],["t","x2",0,1],["q","x1",0,256,512],["s1",0,1],["s1",0,2],["s1",0,0],["c","x2",0,1,"s"],["s1",0,3],["c","x2",0,0,"v"],["q","x2",0,0,512],["t","x1",1,0],["t","x2",1,1],["ch",0,1,"s"],["ch",0,0,"s"],["t","x2",1,0],["c","x1",1,0,"s"],["ch",0,2,"v"],["ch",0,3,"v"],["t","x1",1,1],["q","h",0,256,512],["c","x2",1,1,"s"],["s2",0,3],["q","x1",1,0,256],["c","x2",1,0,"s"],["q","h",0,0,256],["c","x1",1,1,"v"],["s1",1,0],["q","x2",1,0,512],["s1",1,1],["co",0,3,"s"],["s2",0,2],["ch",1,1,"v"],["ch",1,0,"s"],["co",0,2,"s"],["t","x1",2,1],["q","x1",1,256,512],["c","x1",2,1,"s"],["q","h",1,0,256],["t","x1",2,0],["s2",0,0],["s2",0,1],["c","x1",2,0,"v"],["q","x1",2,256,512],["q","x1",2,0,256],["s1",1,2],["co",0,0,"s"],["s1",1,3],["s2",1,1],["ch",1,2,"v"],["st",0,2,4],["t","x2",2,1],["c","x2",2,1,"v"],["co",0,1,"s"],["ch",1,3,"s"],["t","x2",2,0],["s2",1,0],["q","h",1,256,512],["s1",2,2],["c","x2",2,0,"v"],["s1",2,3],["s2",1,3],["ch",2,3,"v"],["co",1,1,"s"],["s2",1,2],["co",1,0,"s"],["s1",2,1],["q","x2",2,0,512],["ch",2,2,"s"],["co",1,3,"s"],["st",0,0,2],["s1",2,0],["q","h",2,256,512],["ch",2,0,"v"],["s2",2,3],["co",1,2,"s"],["ch",2,1,"s"],["co",2,3,"s"],["q","h",2,0,256],["s2",2,2],["st",1,0,2],["st",1,2,4],["st",2,3,4],["s2",2,1],["co",2,2,"v"],["st",2,2,3],["co",2,1,"s"],["st",2,1,2],["s2",2,0],["co",2,0,"s"],["st",2,0,1]]
+STEPS = [["dz",8],["rw",1,"v"],["rw",3,"v"],["t","x1",0,0],["t","x1",0,1],["dz",2],["rw",0,"v"],["t","x2",0,0],["qw",0,256],["c","x1",0,0,"v"],["rw",2,"s"],["c","x1",0,1,"s"],["qw",256,512],["q","x1",0,0,256],["t","x2",0,1],["q","x1",0,256,512],["s1",0,1],["s1",0,2],["s1",0,0],["c","x2",0,1,"s"],["s1",0,3],["c","x2",0,0,"v"],["q","x2",0,0,512],["t","x1",1,0],["t","x2",1,1],["ch",0,1,"s"],["ch",0,0,"s"],["t","x2",1,0],["c","x1",1,0,"s"],["ch",0,2,"v"],["ch",0,3,"v"],["t","x1",1,1],["q","h",0,256,512],["c","x2",1,1,"s"],["s2",0,3],["q","x1",1,0,256],["c","x2",1,0,"s"],["q","h",0,0,256],["c","x1",1,1,"v"],["s1",1,0],["q","x2",1,0,512],["s1",1,1],["co",0,3,"s"],["s2",0,2],["ch",1,1,"v"],["ch",1,0,"s"],["co",0,2,"s"],["t","x1",2,1],["q","x1",1,256,512],["c","x1",2,1,"s"],["q","h",1,0,256],["t","x1",2,0],["s2",0,0],["s2",0,1],["c","x1",2,0,"v"],["q","x1",2,256,512],["q","x1",2,0,256],["s1",1,2],["co",0,0,"s"],["s1",1,3],["s2",1,1],["ch",1,2,"v"],["st",0,2,4],["t","x2",2,1],["c","x2",2,1,"v"],["co",0,1,"s"],["ch",1,3,"s"],["t","x2",2,0],["s2",1,0],["q","h",1,256,512],["s1",2,2],["c","x2",2,0,"v"],["s1",2,3],["s2",1,3],["ch",2,3,"v"],["co",1,1,"s"],["s2",1,2],["co",1,0,"s"],["s1",2,1],["q","x2",2,0,512],["ch",2,2,"s"],["co",1,3,"s"],["st",0,0,2],["s1",2,0],["q","h",2,256,512],["ch",2,0,"v"],["s2",2,3],["co",1,2,"s"],["ch",2,1,"s"],["co",2,3,"s"],["q","h",2,0,256],["s2",2,2],["st",1,0,2],["st",1,2,4],["st",2,3,4],["s2",2,1],["co",2,2,"v"],["st",2,2,3],["co",2,1,"s"],["st",2,1,2],["s2",2,0],["co",2,0,"s"],["st",2,0,1]]
 
 
 def tile_coattentionandcombine_pa_kernel(tc, x1, bi_linear_w, x2, out):
@@ -76,6 +77,11 @@ def tile_coattentionandcombine_pa_kernel(tc, x1, bi_linear_w, x2, out):
         make_identity(nc, ident[:])
 
         banks = {}
+        warm_codes = keep.tile([P, 512], U32, name="warm_codes", align_bytes=64)
+        warm_scales = keep.tile([P, 512], U8, name="warm_scales", align_bytes=64)
+        warm_in = keep.tile([P, 2048], BF16, name="warm_in", align_bytes=64)
+        nc.vector.memset(warm_in[:].bitcast(I32), 0)
+        nc.vector.quantize_mx(out=warm_codes[:].bitcast(FP8X4), scales=warm_scales[:], in_=warm_in[:])
 
         def quantise(s, b, lo, hi):
             nc.vector.quantize_mx(
@@ -86,7 +92,19 @@ def tile_coattentionandcombine_pa_kernel(tc, x1, bi_linear_w, x2, out):
 
         for step in STEPS:
             kind = step[0]
-            if kind == "rw":
+            if kind == "dz":
+                bank = psum.tile([P, 512], F32, tag="bank", name="warm")
+                for r in range(step[1]):
+                    nc.tensor.matmul_mx(
+                        out=bank[:],
+                        lhsT=warm_codes[:, 0:P].bitcast(FP8X4),
+                        lhsT_scale=warm_scales[:, 0:P],
+                        rhs=warm_codes[:].bitcast(FP8X4),
+                        rhs_scale=warm_scales[:],
+                        start=True,
+                        stop=True,
+                    )
+            elif kind == "rw":
                 t, eng = step[1], step[2]
                 u, e = t // 2, t % 2
                 src = w_sb[:].rearrange("p (t u m e) -> p t u m e", t=4, u=2, e=2)[:, :, u, :, e]

@@ -7,7 +7,6 @@ F32 = mybir.dt.float32
 BF16 = mybir.dt.bfloat16
 U32 = mybir.dt.uint32
 U8 = mybir.dt.uint8
-I32 = mybir.dt.int32
 FP8X4 = mybir.dt.float8_e4m3fn_x4
 
 P = 128
@@ -15,8 +14,8 @@ B, L, D = 3, 512, 512
 FLOPS = 2 * 2 * B * L * D * D
 
 PINNED = True
-LOADS = [["w",0,-1],["x1",0,-1],["x2",0,-1],["x1",1,-1],["x2",1,-1],["x1",2,-1],["x2",2,-1]]
-STEPS = [["dz",8],["rw",1,"v"],["rw",3,"v"],["t","x1",0,0],["t","x1",0,1],["dz",2],["rw",0,"v"],["t","x2",0,0],["qw",0,256],["c","x1",0,0,"v"],["rw",2,"s"],["c","x1",0,1,"s"],["qw",256,512],["q","x1",0,0,256],["t","x2",0,1],["q","x1",0,256,512],["s1",0,1],["s1",0,2],["s1",0,0],["c","x2",0,1,"s"],["s1",0,3],["c","x2",0,0,"v"],["q","x2",0,0,512],["t","x1",1,0],["t","x2",1,1],["ch",0,1,"s"],["ch",0,0,"s"],["t","x2",1,0],["c","x1",1,0,"s"],["ch",0,2,"v"],["ch",0,3,"v"],["t","x1",1,1],["q","h",0,256,512],["c","x2",1,1,"s"],["s2",0,3],["q","x1",1,0,256],["c","x2",1,0,"s"],["q","h",0,0,256],["c","x1",1,1,"v"],["s1",1,0],["q","x2",1,0,512],["s1",1,1],["co",0,3,"s"],["s2",0,2],["ch",1,1,"v"],["ch",1,0,"s"],["co",0,2,"s"],["t","x1",2,1],["q","x1",1,256,512],["c","x1",2,1,"s"],["q","h",1,0,256],["t","x1",2,0],["s2",0,0],["s2",0,1],["c","x1",2,0,"v"],["q","x1",2,256,512],["q","x1",2,0,256],["s1",1,2],["co",0,0,"s"],["s1",1,3],["s2",1,1],["ch",1,2,"v"],["st",0,2,4],["t","x2",2,1],["c","x2",2,1,"v"],["co",0,1,"s"],["ch",1,3,"s"],["t","x2",2,0],["s2",1,0],["q","h",1,256,512],["s1",2,2],["c","x2",2,0,"v"],["s1",2,3],["s2",1,3],["ch",2,3,"v"],["co",1,1,"s"],["s2",1,2],["co",1,0,"s"],["s1",2,1],["q","x2",2,0,512],["ch",2,2,"s"],["co",1,3,"s"],["st",0,0,2],["s1",2,0],["q","h",2,256,512],["ch",2,0,"v"],["s2",2,3],["co",1,2,"s"],["ch",2,1,"s"],["co",2,3,"s"],["q","h",2,0,256],["s2",2,2],["st",1,0,2],["st",1,2,4],["st",2,3,4],["s2",2,1],["co",2,2,"v"],["st",2,2,3],["co",2,1,"s"],["st",2,1,2],["s2",2,0],["co",2,0,"s"],["st",2,0,1]]
+LOADS = [["w",0,-1],["x1",0,-1],["x2",0,-1],["x2",2,-1],["x1",1,-1],["x2",1,-1],["x1",2,-1]]
+STEPS = [["rw",3,"v"],["t","x1",0,0],["rw",0,"v"],["rw",1,"v"],["c","x1",0,0,"s"],["t","x1",0,1],["qw",0,256],["rw",2,"v"],["t","x2",0,0],["qw",256,512],["t","x2",0,1],["c","x1",0,1,"s"],["q","x1",0,0,256],["q","x1",0,256,512],["c","x2",0,1,"v"],["c","x2",0,0,"s"],["s1",0,0],["s1",0,1],["q","x2",0,0,512],["ch",0,0,"s"],["ch",0,1,"s"],["s1",0,3],["ch",0,3,"v"],["s1",0,2],["t","x2",2,0],["t","x1",1,1],["q","h",0,0,256],["t","x1",1,0],["c","x2",2,0,"v"],["t","x2",2,1],["ch",0,2,"s"],["s2",0,0],["t","x2",1,0],["q","h",0,256,512],["t","x2",1,1],["c","x1",1,1,"s"],["c","x2",2,1,"v"],["c","x1",1,0,"s"],["q","x1",1,0,256],["s2",0,1],["s1",1,0],["q","x1",1,256,512],["c","x2",1,1,"v"],["t","x1",2,1],["co",0,0,"s"],["c","x2",1,0,"s"],["co",0,1,"s"],["s1",1,2],["st",0,1,2],["q","x2",1,0,512],["st",0,0,1],["ch",1,0,"s"],["s1",1,1],["c","x1",2,1,"v"],["s1",1,3],["q","h",1,0,128],["s2",0,2],["ch",1,2,"s"],["ch",1,1,"s"],["co",0,2,"s"],["s2",0,3],["t","x1",2,0],["q","x1",2,256,512],["c","x1",2,0,"s"],["ch",1,3,"v"],["q","h",1,128,256],["co",0,3,"v"],["q","h",1,384,512],["q","h",1,256,384],["s2",1,0],["s1",2,2],["s2",1,1],["s2",1,3],["co",1,0,"s"],["st",0,2,3],["s2",1,2],["q","x1",2,0,256],["s1",2,3],["ch",2,2,"s"],["s1",2,0],["co",1,1,"v"],["q","x2",2,0,512],["st",0,3,4],["s1",2,1],["co",1,3,"s"],["co",1,2,"s"],["q","h",2,256,384],["st",1,0,1],["ch",2,3,"v"],["ch",2,0,"s"],["st",1,1,2],["q","h",2,384,512],["s2",2,2],["q","h",2,0,128],["st",1,3,4],["st",1,2,3],["s2",2,3],["co",2,2,"s"],["ch",2,1,"v"],["st",2,2,3],["q","h",2,128,256],["s2",2,0],["s2",2,1],["co",2,3,"s"],["st",2,3,4],["co",2,0,"s"],["co",2,1,"s"],["st",2,0,1],["st",2,1,2]]
 
 
 def tile_coattentionandcombine_pa_kernel(tc, x1, bi_linear_w, x2, out):
@@ -77,11 +76,6 @@ def tile_coattentionandcombine_pa_kernel(tc, x1, bi_linear_w, x2, out):
         make_identity(nc, ident[:])
 
         banks = {}
-        warm_codes = keep.tile([P, 512], U32, name="warm_codes", align_bytes=64)
-        warm_scales = keep.tile([P, 512], U8, name="warm_scales", align_bytes=64)
-        warm_in = keep.tile([P, 2048], BF16, name="warm_in", align_bytes=64)
-        nc.vector.memset(warm_in[:].bitcast(I32), 0)
-        nc.vector.quantize_mx(out=warm_codes[:].bitcast(FP8X4), scales=warm_scales[:], in_=warm_in[:])
 
         def quantise(s, b, lo, hi):
             nc.vector.quantize_mx(
@@ -92,19 +86,7 @@ def tile_coattentionandcombine_pa_kernel(tc, x1, bi_linear_w, x2, out):
 
         for step in STEPS:
             kind = step[0]
-            if kind == "dz":
-                bank = psum.tile([P, 512], F32, tag="bank", name="warm")
-                for r in range(step[1]):
-                    nc.tensor.matmul_mx(
-                        out=bank[:],
-                        lhsT=warm_codes[:, 0:P].bitcast(FP8X4),
-                        lhsT_scale=warm_scales[:, 0:P],
-                        rhs=warm_codes[:].bitcast(FP8X4),
-                        rhs_scale=warm_scales[:],
-                        start=True,
-                        stop=True,
-                    )
-            elif kind == "rw":
+            if kind == "rw":
                 t, eng = step[1], step[2]
                 u, e = t // 2, t % 2
                 src = w_sb[:].rearrange("p (t u m e) -> p t u m e", t=4, u=2, e=2)[:, :, u, :, e]

@@ -14,8 +14,8 @@ B, L, D = 3, 512, 512
 FLOPS = 2 * 2 * B * L * D * D
 
 PINNED = True
-LOADS = [["w",0,-1],["x1",0,-1],["x2",0,-1],["x2",2,-1],["x1",1,-1],["x2",1,-1],["x1",2,-1]]
-STEPS = [["rw",3,"v"],["t","x1",0,0],["rw",0,"v"],["rw",1,"v"],["c","x1",0,0,"s"],["t","x1",0,1],["qw",0,256],["rw",2,"v"],["t","x2",0,0],["qw",256,512],["t","x2",0,1],["c","x1",0,1,"s"],["q","x1",0,0,256],["q","x1",0,256,512],["c","x2",0,1,"v"],["c","x2",0,0,"s"],["s1",0,0],["s1",0,1],["q","x2",0,0,512],["ch",0,0,"s"],["ch",0,1,"s"],["s1",0,3],["ch",0,3,"v"],["s1",0,2],["t","x2",2,0],["t","x1",1,1],["q","h",0,0,256],["t","x1",1,0],["c","x2",2,0,"v"],["t","x2",2,1],["ch",0,2,"s"],["s2",0,0],["t","x2",1,0],["q","h",0,256,512],["t","x2",1,1],["c","x1",1,1,"s"],["c","x2",2,1,"v"],["c","x1",1,0,"s"],["q","x1",1,0,256],["s2",0,1],["s1",1,0],["q","x1",1,256,512],["c","x2",1,1,"v"],["t","x1",2,1],["co",0,0,"s"],["c","x2",1,0,"s"],["co",0,1,"s"],["s1",1,2],["st",0,1,2],["q","x2",1,0,512],["st",0,0,1],["ch",1,0,"s"],["s1",1,1],["c","x1",2,1,"v"],["s1",1,3],["q","h",1,0,128],["s2",0,2],["ch",1,2,"s"],["ch",1,1,"s"],["co",0,2,"s"],["s2",0,3],["t","x1",2,0],["q","x1",2,256,512],["c","x1",2,0,"s"],["ch",1,3,"v"],["q","h",1,128,256],["co",0,3,"v"],["q","h",1,384,512],["q","h",1,256,384],["s2",1,0],["s1",2,2],["s2",1,1],["s2",1,3],["co",1,0,"s"],["st",0,2,3],["s2",1,2],["q","x1",2,0,256],["s1",2,3],["ch",2,2,"s"],["s1",2,0],["co",1,1,"v"],["q","x2",2,0,512],["st",0,3,4],["s1",2,1],["co",1,3,"s"],["co",1,2,"s"],["q","h",2,256,384],["st",1,0,1],["ch",2,3,"v"],["ch",2,0,"s"],["st",1,1,2],["q","h",2,384,512],["s2",2,2],["q","h",2,0,128],["st",1,3,4],["st",1,2,3],["s2",2,3],["co",2,2,"s"],["ch",2,1,"v"],["st",2,2,3],["q","h",2,128,256],["s2",2,0],["s2",2,1],["co",2,3,"s"],["st",2,3,4],["co",2,0,"s"],["co",2,1,"s"],["st",2,0,1],["st",2,1,2]]
+LOADS = [["w",0,-1],["x1",0,-1],["x2",0,-1],["x2",1,-1],["x1",1,-1],["x1",2,-1],["x2",2,-1]]
+STEPS = [["rw",1,"s"],["rw",2,"v"],["rw",3,"v"],["rw",0,"v"],["t","x1",0,1],["t","x1",0,0],["qw",256,512],["qw",0,256],["c","x1",0,1,"v"],["t","x2",0,1],["c","x1",0,0,"s"],["q","x1",0,256,512],["t","x2",0,0],["q","x1",0,0,256],["c","x2",0,1,"v"],["c","x2",0,0,"s"],["s1",0,3],["q","x2",0,0,512],["s1",0,0],["s1",0,2],["s1",0,1],["ch",0,0,"s"],["ch",0,3,"v"],["t","x1",1,1],["ch",0,2,"s"],["t","x2",1,1],["ch",0,1,"v"],["q","h",0,256,512],["c","x1",1,1,"s"],["t","x1",1,0],["c","x1",1,0,"s"],["s2",0,3],["q","h",0,0,256],["c","x2",1,1,"s"],["q","x1",1,256,512],["s2",0,0],["q","x1",1,0,256],["s2",0,2],["s2",0,1],["co",0,3,"v"],["s1",1,1],["co",0,0,"s"],["co",0,2,"v"],["s1",1,0],["s1",1,3],["co",0,1,"v"],["st",0,0,1],["ch",1,1,"s"],["ch",1,0,"v"],["q","h",1,128,256],["t","x1",2,1],["st",0,3,4],["t","x2",1,0],["ch",1,3,"s"],["c","x1",2,1,"s"],["t","x2",2,0],["t","x2",2,1],["t","x1",2,0],["c","x2",1,0,"v"],["q","h",1,384,512],["q","x2",1,0,512],["c","x2",2,0,"s"],["c","x2",2,1,"s"],["s1",1,2],["q","x1",2,256,512],["q","h",1,0,128],["st",0,1,2],["s2",1,1],["s2",1,3],["q","x2",2,0,512],["c","x1",2,0,"s"],["q","x1",2,0,256],["st",0,2,3],["ch",1,2,"s"],["s1",2,2],["s2",1,0],["co",1,1,"v"],["co",1,3,"s"],["s1",2,0],["q","h",1,256,384],["ch",2,2,"v"],["st",1,3,4],["co",1,0,"s"],["q","h",2,256,384],["ch",2,0,"s"],["s1",2,1],["s2",1,2],["ch",2,1,"v"],["q","h",2,0,128],["s1",2,3],["s2",2,2],["q","h",2,128,256],["st",1,0,1],["co",1,2,"s"],["st",1,1,2],["s2",2,0],["s2",2,1],["st",1,2,3],["ch",2,3,"s"],["co",2,2,"v"],["st",2,2,3],["q","h",2,384,512],["s2",2,3],["co",2,0,"s"],["co",2,3,"s"],["co",2,1,"v"],["st",2,0,1],["st",2,1,2],["st",2,3,4]]
 
 
 def tile_coattentionandcombine_pa_kernel(tc, x1, bi_linear_w, x2, out):

@@ -10,167 +10,186 @@ U8 = mybir.dt.uint8
 FP8X4 = mybir.dt.float8_e4m3fn_x4
 
 P = 128
+PACK = 4
 B, L, D = 3, 512, 512
+BANK = 512
+N_BANKS = 8
 FLOPS = 2 * 2 * B * L * D * D
-
-PINNED = True
-LOADS = [["w",0,-1],["x1",0,-1],["x2",0,-1],["x2",1,-1],["x1",1,-1],["x1",2,-1],["x2",2,-1]]
-STEPS = [["rw",1,"s"],["rw",2,"v"],["rw",3,"v"],["rw",0,"v"],["t","x1",0,1],["t","x1",0,0],["qw",256,512],["qw",0,256],["c","x1",0,1,"v"],["t","x2",0,1],["c","x1",0,0,"s"],["q","x1",0,256,512],["t","x2",0,0],["q","x1",0,0,256],["c","x2",0,1,"v"],["c","x2",0,0,"s"],["s1",0,3],["q","x2",0,0,512],["s1",0,0],["s1",0,2],["s1",0,1],["ch",0,0,"s"],["ch",0,3,"v"],["t","x1",1,1],["ch",0,2,"s"],["t","x2",1,1],["ch",0,1,"v"],["q","h",0,256,512],["c","x1",1,1,"s"],["t","x1",1,0],["c","x1",1,0,"s"],["s2",0,3],["q","h",0,0,256],["c","x2",1,1,"s"],["q","x1",1,256,512],["s2",0,0],["q","x1",1,0,256],["s2",0,2],["s2",0,1],["co",0,3,"v"],["s1",1,1],["co",0,0,"s"],["co",0,2,"v"],["s1",1,0],["s1",1,3],["co",0,1,"v"],["st",0,0,1],["ch",1,1,"s"],["ch",1,0,"v"],["q","h",1,128,256],["t","x1",2,1],["st",0,3,4],["t","x2",1,0],["ch",1,3,"s"],["c","x1",2,1,"s"],["t","x2",2,0],["t","x2",2,1],["t","x1",2,0],["c","x2",1,0,"v"],["q","h",1,384,512],["q","x2",1,0,512],["c","x2",2,0,"s"],["c","x2",2,1,"s"],["s1",1,2],["q","x1",2,256,512],["q","h",1,0,128],["st",0,1,2],["s2",1,1],["s2",1,3],["q","x2",2,0,512],["c","x1",2,0,"s"],["q","x1",2,0,256],["st",0,2,3],["ch",1,2,"s"],["s1",2,2],["s2",1,0],["co",1,1,"v"],["co",1,3,"s"],["s1",2,0],["q","h",1,256,384],["ch",2,2,"v"],["st",1,3,4],["co",1,0,"s"],["q","h",2,256,384],["ch",2,0,"s"],["s1",2,1],["s2",1,2],["ch",2,1,"v"],["q","h",2,0,128],["s1",2,3],["s2",2,2],["q","h",2,128,256],["st",1,0,1],["co",1,2,"s"],["st",1,1,2],["s2",2,0],["s2",2,1],["st",1,2,3],["ch",2,3,"s"],["co",2,2,"v"],["st",2,2,3],["q","h",2,384,512],["s2",2,3],["co",2,0,"s"],["co",2,3,"s"],["co",2,1,"v"],["st",2,0,1],["st",2,1,2],["st",2,3,4]]
 
 
 def tile_coattentionandcombine_pa_kernel(tc, x1, bi_linear_w, x2, out):
     nc = tc.nc
     with ExitStack() as ctx:
-        keep = ctx.enter_context(tc.tile_pool(name="keep", bufs=1))
-        psum = ctx.enter_context(tc.psum_pool(name="psum", bufs=8))
-        if PINNED:
-            ctx.enter_context(tc.manual_schedule())
+        sbuf = ctx.enter_context(tc.tile_pool(name="sbuf", bufs=1))
+        psum = ctx.enter_context(tc.psum_pool(name="psum", bufs=N_BANKS))
+        ctx.enter_context(tc.manual_schedule())
 
-        def copy(eng, dst, src):
-            if eng == "v":
+        def quantisable(name, columns):
+            return (
+                sbuf.tile([P, columns * PACK], BF16, name=name + "_grouped", align_bytes=64),
+                sbuf.tile([P, columns], U32, name=name + "_words", align_bytes=64),
+                sbuf.tile([P, columns], U8, name=name + "_scales", align_bytes=64),
+            )
+
+        def quantise(operand, first, last):
+            grouped, words, scales = operand
+            nc.vector.quantize_mx(
+                out=words[:, first:last].bitcast(FP8X4),
+                scales=scales[:, first:last],
+                in_=grouped[:, first * PACK : last * PACK],
+            )
+
+        def copy(engine, dst, src):
+            if engine == "vector":
                 nc.vector.tensor_copy(out=dst, in_=src)
             else:
                 nc.scalar.copy(out=dst, in_=src)
 
-        w_sb = keep.tile([P, 4 * D], BF16, name="w_sb")
-        w_grp = keep.tile([P, 4 * D], BF16, name="w_grp", align_bytes=64)
-        w_codes = keep.tile([P, D], U32, name="w_codes", align_bytes=64)
-        w_scales = keep.tile([P, D], U8, name="w_scales", align_bytes=64)
-        ident = keep.tile([P, P], F32, name="ident")
-        raw = {}
-        grp = {}
-        codes = {}
-        scales = {}
-        for b in range(B):
-            for s in ("x1", "x2", "h"):
-                if s != "h":
-                    raw[(s, b)] = keep.tile([P, 4 * D], BF16, name="%s_raw%d" % (s, b))
-                grp[(s, b)] = keep.tile([P, 4 * L], BF16, name="%s_grp%d" % (s, b), align_bytes=64)
-                codes[(s, b)] = keep.tile([P, L], U32, name="%s_codes%d" % (s, b), align_bytes=64)
-                scales[(s, b)] = keep.tile([P, L], U8, name="%s_scales%d" % (s, b), align_bytes=64)
-        out_sb = [keep.tile([P, 4 * L], F32, name="out_sb%d" % b) for b in range(B)]
+        w_rows = sbuf.tile([P, PACK * D], BF16, name="w_rows")
+        w_mx = quantisable("w", D)
+        x_rows = [sbuf.tile([P, PACK * D], BF16, name="x_rows%d" % r) for r in range(2 * B)]
+        x_mx = [quantisable("x%d" % r, L) for r in range(2 * B)]
+        h_mx = [quantisable("h%d" % b, L) for b in range(B)]
+        out_rows = [sbuf.tile([P, PACK * L], F32, name="out_rows%d" % b) for b in range(B)]
+        identity = sbuf.tile([P, P], F32, name="identity")
 
-        for s, b, g in LOADS:
-            if s == "w":
-                nc.sync.dma_start(
-                    out=w_sb[:].rearrange("p (u r) -> p u r", u=2),
-                    in_=bi_linear_w.rearrange("(u p e) c -> p u (e c)", u=2, e=2),
-                )
-            elif s == "x1" and g < 0:
-                nc.sync.dma_start(out=raw[(s, b)][:], in_=x1[b].rearrange("(q i) d -> q (i d)", i=4))
-            elif s == "x1":
-                nc.sync.dma_start(
-                    out=raw[(s, b)][:, g * 1024 : (g + 1) * 1024],
-                    in_=x1[b].rearrange("(q i) d -> q (i d)", i=4)[:, g * 1024 : (g + 1) * 1024],
-                )
-            elif g >= 0:
-                nc.sync.dma_start(
-                    out=raw[(s, b)][:, g * 1024 : (g + 1) * 1024],
-                    in_=x2[b, g * 256 : (g + 1) * 256, :].rearrange("(q i) d -> q (i d)", i=2),
-                )
-            else:
-                nc.sync.dma_start(
-                    out=raw[(s, b)][:].rearrange("p (h r) -> p h r", h=2),
-                    in_=x2[b].rearrange("(h q i) d -> q h (i d)", h=2, i=2),
-                )
-        make_identity(nc, ident[:])
+        nc.sync.dma_start(
+            out=w_rows[:].rearrange("p (u r) -> p u r", u=2),
+            in_=bi_linear_w.rearrange("(u p e) c -> p u (e c)", u=2, e=2),
+        )
+        for b in range(B):
+            nc.sync.dma_start(out=x_rows[2 * b][:], in_=x1[b].rearrange("(q i) d -> q (i d)", i=4))
+            nc.sync.dma_start(
+                out=x_rows[2 * b + 1][:].rearrange("p (h r) -> p h r", h=2),
+                in_=x2[b].rearrange("(h q i) d -> q h (i d)", h=2, i=2),
+            )
+        make_identity(nc, identity[:])
 
         banks = {}
 
-        def quantise(s, b, lo, hi):
-            nc.vector.quantize_mx(
-                out=codes[(s, b)][:, lo:hi].bitcast(FP8X4),
-                scales=scales[(s, b)][:, lo:hi],
-                in_=grp[(s, b)][:, 4 * lo : 4 * hi],
+        def regroup_w(t, engine):
+            columns = w_rows[:].rearrange("p (k u m e) -> p k u m e", k=PACK, u=2, e=2)[:, :, t // 2, :, t % 2]
+            copy(
+                engine,
+                w_mx[0][:, t * P * PACK : (t + 1) * P * PACK].rearrange("p (m k) -> p m k", k=PACK),
+                columns.rearrange("p k m -> p m k"),
             )
 
-        for step in STEPS:
-            kind = step[0]
-            if kind == "rw":
-                t, eng = step[1], step[2]
-                u, e = t // 2, t % 2
-                src = w_sb[:].rearrange("p (t u m e) -> p t u m e", t=4, u=2, e=2)[:, :, u, :, e]
-                copy(
-                    eng,
-                    w_grp[:, t * 512 : (t + 1) * 512].rearrange("p (m t) -> p m t", t=4),
-                    src.rearrange("p t m -> p m t"),
-                )
-            elif kind == "qw":
-                lo, hi = step[1], step[2]
-                nc.vector.quantize_mx(
-                    out=w_codes[:, lo:hi].bitcast(FP8X4),
-                    scales=w_scales[:, lo:hi],
-                    in_=w_grp[:, 4 * lo : 4 * hi],
-                )
-            elif kind == "t":
-                s, b, g = step[1], step[2], step[3]
-                words = raw[(s, b)][:].bitcast(F32)
-                bank = psum.tile([P, 512], F32, tag="bank", name="t_%s%d%d" % (s, b, g))
-                for a in range(4):
+        def transpose_x(r):
+            pairs = x_rows[r][:].bitcast(F32)
+            for half in range(2):
+                bank = psum.tile([P, BANK], F32, tag="bank", name="x_bank")
+                for block in range(4):
                     nc.tensor.transpose(
-                        bank[:, a * P : (a + 1) * P],
-                        words[:, g * 512 + a * P : g * 512 + (a + 1) * P],
-                        ident[:],
+                        bank[:, block * P : (block + 1) * P],
+                        pairs[:, half * BANK + block * P : half * BANK + (block + 1) * P],
+                        identity[:],
                     )
-                banks[("t", s, b, g)] = bank
-            elif kind == "c":
-                s, b, g, eng = step[1], step[2], step[3], step[4]
-                bank = banks[("t", s, b, g)]
-                dst = grp[(s, b)][:].bitcast(F32)[:, g * 512 : (g + 1) * 512]
-                if s == "x1":
-                    copy(
-                        eng,
-                        dst.rearrange("p (i q u) -> p i q u", i=2, u=2),
-                        bank[:].rearrange("p (i u q) -> p i q u", i=2, u=2),
-                    )
-                else:
-                    copy(
-                        eng,
-                        dst.rearrange("p (q a) -> p q a", a=4),
-                        bank[:].rearrange("p (a q) -> p q a", a=4),
-                    )
-            elif kind == "q":
-                quantise(step[1], step[2], step[3], step[4])
-            elif kind == "s1":
-                b, i = step[1], step[2]
-                bank = psum.tile([P, 512], F32, tag="bank", name="h_%d%d" % (b, i))
-                for t in range(4):
+                banks[("x", r, half)] = bank
+
+        def regroup_x(r, half, engine):
+            bank = banks[("x", r, half)]
+            grouped = x_mx[r][0][:].bitcast(F32)[:, half * BANK : (half + 1) * BANK]
+            if r % 2 == 0:
+                copy(
+                    engine,
+                    grouped.rearrange("p (i q u) -> p i q u", i=2, u=2),
+                    bank[:].rearrange("p (i u q) -> p i q u", i=2, u=2),
+                )
+            else:
+                copy(
+                    engine,
+                    grouped.rearrange("p (q block) -> p q block", block=4),
+                    bank[:].rearrange("p (block q) -> p q block", block=4),
+                )
+
+        def quantise_x(r):
+            if r % 2 == 0:
+                quantise(x_mx[r], 0, L // 2)
+                quantise(x_mx[r], L // 2, L)
+            else:
+                quantise(x_mx[r], 0, L)
+
+        def tiles_of(j):
+            return [(j // 2, 2 * (j % 2)), (j // 2, 2 * (j % 2) + 1)]
+
+        def first_matmul(j):
+            for b, i in tiles_of(j):
+                bank = psum.tile([P, BANK], F32, tag="bank", name="h_bank")
+                for t in range(PACK):
                     nc.tensor.matmul_mx(
                         out=bank[:, t * P : (t + 1) * P],
-                        lhsT=w_codes[:, t * P : (t + 1) * P].bitcast(FP8X4),
-                        lhsT_scale=w_scales[:, t * P : (t + 1) * P],
-                        rhs=codes[("x1", b)][:, i * P : (i + 1) * P].bitcast(FP8X4),
-                        rhs_scale=scales[("x1", b)][:, i * P : (i + 1) * P],
+                        lhsT=w_mx[1][:, t * P : (t + 1) * P].bitcast(FP8X4),
+                        lhsT_scale=w_mx[2][:, t * P : (t + 1) * P],
+                        rhs=x_mx[2 * b][1][:, i * P : (i + 1) * P].bitcast(FP8X4),
+                        rhs_scale=x_mx[2 * b][2][:, i * P : (i + 1) * P],
                         start=True,
                         stop=True,
                     )
                 banks[("h", b, i)] = bank
-            elif kind == "ch":
-                b, i, eng = step[1], step[2], step[3]
-                copy(
-                    eng,
-                    grp[("h", b)][:, i * 512 : (i + 1) * 512].rearrange("p (q t) -> p q t", t=4),
-                    banks[("h", b, i)][:].rearrange("p (t q) -> p q t", t=4),
-                )
-            elif kind == "s2":
-                b, i = step[1], step[2]
-                bank = psum.tile([P, 512], F32, tag="bank", name="o_%d%d" % (b, i))
+
+        def round_h(b, i, engine):
+            copy(
+                engine,
+                h_mx[b][0][:, i * P * PACK : (i + 1) * P * PACK].rearrange("p (q t) -> p q t", t=PACK),
+                banks[("h", b, i)][:].rearrange("p (t q) -> p q t", t=PACK),
+            )
+
+        def second_matmul(j):
+            for b, i in tiles_of(j):
+                bank = psum.tile([P, BANK], F32, tag="bank", name="sim_bank")
                 nc.tensor.matmul_mx(
                     out=bank[:],
-                    lhsT=codes[("h", b)][:, i * P : (i + 1) * P].bitcast(FP8X4),
-                    lhsT_scale=scales[("h", b)][:, i * P : (i + 1) * P],
-                    rhs=codes[("x2", b)][:].bitcast(FP8X4),
-                    rhs_scale=scales[("x2", b)][:],
+                    lhsT=h_mx[b][1][:, i * P : (i + 1) * P].bitcast(FP8X4),
+                    lhsT_scale=h_mx[b][2][:, i * P : (i + 1) * P],
+                    rhs=x_mx[2 * b + 1][1][:].bitcast(FP8X4),
+                    rhs_scale=x_mx[2 * b + 1][2][:],
                     start=True,
                     stop=True,
                 )
-                banks[("o", b, i)] = bank
-            elif kind == "co":
-                b, i, eng = step[1], step[2], step[3]
-                copy(eng, out_sb[b][:, i * 512 : (i + 1) * 512], banks[("o", b, i)][:])
-            elif kind == "st":
-                b, lo, hi = step[1], step[2], step[3]
-                nc.sync.dma_start(
-                    out=out[b].rearrange("(q i) m -> q (i m)", i=4)[:, lo * 512 : hi * 512],
-                    in_=out_sb[b][:, lo * 512 : hi * 512],
-                )
+                banks[("sim", b, i)] = bank
+
+        def store_sim(b, i, engine):
+            copy(engine, out_rows[b][:, i * L : (i + 1) * L], banks[("sim", b, i)][:])
+            nc.sync.dma_start(
+                out=out[b].rearrange("(q i) m -> q (i m)", i=4)[:, i * L : (i + 1) * L],
+                in_=out_rows[b][:, i * L : (i + 1) * L],
+            )
+
+        for t in range(PACK):
+            regroup_w(t, "scalar" if t == PACK - 1 else "vector")
+        quantise(w_mx, 0, D // 2)
+        quantise(w_mx, D // 2, D)
+        transpose_x(0)
+        transpose_x(1)
+        regroup_x(0, 0, "scalar")
+        regroup_x(0, 1, "scalar")
+        quantise_x(0)
+        regroup_x(1, 0, "scalar")
+        regroup_x(1, 1, "vector")
+        quantise_x(1)
+        first_matmul(0)
+        transpose_x(2)
+
+        steps = 2 * B
+        for j in range(steps + 1):
+            if j < steps:
+                for b, i in tiles_of(j):
+                    round_h(b, i, "scalar")
+            if j > 0:
+                (b, i), (b_next, i_next) = tiles_of(j - 1)
+                store_sim(b, i, "vector")
+                store_sim(b_next, i_next, "scalar")
+            if j < steps:
+                for b, i in tiles_of(j):
+                    quantise(h_mx[b], i * P, (i + 1) * P)
+            if j + 2 < 2 * B:
+                regroup_x(j + 2, 0, "scalar")
+                regroup_x(j + 2, 1, "vector")
+                quantise_x(j + 2)
+            if j + 1 < steps:
+                first_matmul(j + 1)
+            if j < steps:
+                second_matmul(j)
+            if j + 3 < 2 * B:
+                transpose_x(j + 3)

@@ -128,12 +128,17 @@ def tile_coattentionandcombine_pa_kernel(tc, x1, bi_linear_w, x2, out):
                     )
                 banks[("h", b, i)] = bank
 
-        def round_h(b, i, engine):
+        def round_h(tile, engine):
+            b, i = tile
             copy(
                 engine,
                 h_mx[b][0][:, i * P * PACK : (i + 1) * P * PACK].rearrange("p (q t) -> p q t", t=PACK),
                 banks[("h", b, i)][:].rearrange("p (t q) -> p q t", t=PACK),
             )
+
+        def quantise_h(tile):
+            b, i = tile
+            quantise(h_mx[b], i * P, (i + 1) * P)
 
         def second_matmul(j):
             for b, i in tiles_of(j):
@@ -149,7 +154,8 @@ def tile_coattentionandcombine_pa_kernel(tc, x1, bi_linear_w, x2, out):
                 )
                 banks[("sim", b, i)] = bank
 
-        def store_sim(b, i, engine):
+        def store_sim(tile, engine):
+            b, i = tile
             copy(engine, out_rows[b][:, i * L : (i + 1) * L], banks[("sim", b, i)][:])
             nc.sync.dma_start(
                 out=out[b].rearrange("(q i) m -> q (i m)", i=4)[:, i * L : (i + 1) * L],
@@ -173,16 +179,20 @@ def tile_coattentionandcombine_pa_kernel(tc, x1, bi_linear_w, x2, out):
 
         steps = 2 * B
         for j in range(steps + 1):
+            last_step = j == steps - 1
             if j < steps:
-                for b, i in tiles_of(j):
-                    round_h(b, i, "scalar")
+                tile_a, tile_b = tiles_of(j)
+                round_h(tile_a, "scalar")
+                round_h(tile_b, "vector" if last_step else "scalar")
+                quantise_h(tile_a)
+                if last_step:
+                    quantise_h(tile_b)
             if j > 0:
-                (b, i), (b_next, i_next) = tiles_of(j - 1)
-                store_sim(b, i, "vector")
-                store_sim(b_next, i_next, "scalar")
-            if j < steps:
-                for b, i in tiles_of(j):
-                    quantise(h_mx[b], i * P, (i + 1) * P)
+                ready_a, ready_b = tiles_of(j - 1)
+                store_sim(ready_a, "scalar")
+                store_sim(ready_b, "vector")
+            if j < steps - 1:
+                quantise_h(tile_b)
             if j + 2 < 2 * B:
                 regroup_x(j + 2, 0, "scalar")
                 regroup_x(j + 2, 1, "vector")

from contextlib import ExitStack

import concourse.mybir as mybir
from concourse.masks import make_identity

F32 = mybir.dt.float32
BF16 = mybir.dt.bfloat16
U32 = mybir.dt.uint32
U8 = mybir.dt.uint8
FP8X4 = mybir.dt.float8_e4m3fn_x4

P = 128
PACK = 4
B, L, D = 3, 512, 512
BANK = 512
N_BANKS = 8
FLOPS = 2 * 2 * B * L * D * D


def tile_coattentionandcombine_pa_kernel(tc, x1, bi_linear_w, x2, out):
    nc = tc.nc
    with ExitStack() as ctx:
        sbuf = ctx.enter_context(tc.tile_pool(name="sbuf", bufs=1))
        psum = ctx.enter_context(tc.psum_pool(name="psum", bufs=N_BANKS))
        ctx.enter_context(tc.manual_schedule())

        def quantisable(name, columns):
            return (
                sbuf.tile([P, columns * PACK], BF16, name=name + "_grouped", align_bytes=64),
                sbuf.tile([P, columns], U32, name=name + "_words", align_bytes=64),
                sbuf.tile([P, columns], U8, name=name + "_scales", align_bytes=64),
            )

        def quantise(operand, first, last):
            grouped, words, scales = operand
            nc.vector.quantize_mx(
                out=words[:, first:last].bitcast(FP8X4),
                scales=scales[:, first:last],
                in_=grouped[:, first * PACK : last * PACK],
            )

        def copy(engine, dst, src):
            if engine == "vector":
                nc.vector.tensor_copy(out=dst, in_=src)
            else:
                nc.scalar.copy(out=dst, in_=src)

        w_rows = sbuf.tile([P, PACK * D], BF16, name="w_rows")
        w_mx = quantisable("w", D)
        x_rows = [sbuf.tile([P, PACK * D], BF16, name="x_rows%d" % r) for r in range(2 * B)]
        x_mx = [quantisable("x%d" % r, L) for r in range(2 * B)]
        h_mx = [quantisable("h%d" % b, L) for b in range(B)]
        out_rows = [sbuf.tile([P, PACK * L], F32, name="out_rows%d" % b) for b in range(B)]
        identity = sbuf.tile([P, P], F32, name="identity")

        nc.sync.dma_start(
            out=w_rows[:].rearrange("p (u r) -> p u r", u=2),
            in_=bi_linear_w.rearrange("(u p e) c -> p u (e c)", u=2, e=2),
        )
        for b in range(B):
            nc.sync.dma_start(out=x_rows[2 * b][:], in_=x1[b].rearrange("(q i) d -> q (i d)", i=4))
            nc.sync.dma_start(
                out=x_rows[2 * b + 1][:].rearrange("p (h r) -> p h r", h=2),
                in_=x2[b].rearrange("(h q i) d -> q h (i d)", h=2, i=2),
            )
        make_identity(nc, identity[:])

        banks = {}

        def regroup_w(t, engine):
            columns = w_rows[:].rearrange("p (k u m e) -> p k u m e", k=PACK, u=2, e=2)[:, :, t // 2, :, t % 2]
            copy(
                engine,
                w_mx[0][:, t * P * PACK : (t + 1) * P * PACK].rearrange("p (m k) -> p m k", k=PACK),
                columns.rearrange("p k m -> p m k"),
            )

        def transpose_x(r):
            pairs = x_rows[r][:].bitcast(F32)
            for half in range(2):
                bank = psum.tile([P, BANK], F32, tag="bank", name="x_bank")
                for block in range(4):
                    nc.tensor.transpose(
                        bank[:, block * P : (block + 1) * P],
                        pairs[:, half * BANK + block * P : half * BANK + (block + 1) * P],
                        identity[:],
                    )
                banks[("x", r, half)] = bank

        def regroup_x(r, half, engine):
            bank = banks[("x", r, half)]
            grouped = x_mx[r][0][:].bitcast(F32)[:, half * BANK : (half + 1) * BANK]
            if r % 2 == 0:
                copy(
                    engine,
                    grouped.rearrange("p (i q u) -> p i q u", i=2, u=2),
                    bank[:].rearrange("p (i u q) -> p i q u", i=2, u=2),
                )
            else:
                copy(
                    engine,
                    grouped.rearrange("p (q block) -> p q block", block=4),
                    bank[:].rearrange("p (block q) -> p q block", block=4),
                )

        def quantise_x(r):
            if r % 2 == 0:
                quantise(x_mx[r], 0, L // 2)
                quantise(x_mx[r], L // 2, L)
            else:
                quantise(x_mx[r], 0, L)

        def tiles_of(j):
            return [(j // 2, 2 * (j % 2)), (j // 2, 2 * (j % 2) + 1)]

        def first_matmul(j):
            for b, i in tiles_of(j):
                bank = psum.tile([P, BANK], F32, tag="bank", name="h_bank")
                for t in range(PACK):
                    nc.tensor.matmul_mx(
                        out=bank[:, t * P : (t + 1) * P],
                        lhsT=w_mx[1][:, t * P : (t + 1) * P].bitcast(FP8X4),
                        lhsT_scale=w_mx[2][:, t * P : (t + 1) * P],
                        rhs=x_mx[2 * b][1][:, i * P : (i + 1) * P].bitcast(FP8X4),
                        rhs_scale=x_mx[2 * b][2][:, i * P : (i + 1) * P],
                        start=True,
                        stop=True,
                    )
                banks[("h", b, i)] = bank

        def round_h(tile, engine):
            b, i = tile
            copy(
                engine,
                h_mx[b][0][:, i * P * PACK : (i + 1) * P * PACK].rearrange("p (q t) -> p q t", t=PACK),
                banks[("h", b, i)][:].rearrange("p (t q) -> p q t", t=PACK),
            )

        def quantise_h(tile):
            b, i = tile
            quantise(h_mx[b], i * P, (i + 1) * P)

        def second_matmul(j):
            for b, i in tiles_of(j):
                bank = psum.tile([P, BANK], F32, tag="bank", name="sim_bank")
                nc.tensor.matmul_mx(
                    out=bank[:],
                    lhsT=h_mx[b][1][:, i * P : (i + 1) * P].bitcast(FP8X4),
                    lhsT_scale=h_mx[b][2][:, i * P : (i + 1) * P],
                    rhs=x_mx[2 * b + 1][1][:].bitcast(FP8X4),
                    rhs_scale=x_mx[2 * b + 1][2][:],
                    start=True,
                    stop=True,
                )
                banks[("sim", b, i)] = bank

        def store_sim(tile, engine):
            b, i = tile
            copy(engine, out_rows[b][:, i * L : (i + 1) * L], banks[("sim", b, i)][:])
            nc.sync.dma_start(
                out=out[b].rearrange("(q i) m -> q (i m)", i=4)[:, i * L : (i + 1) * L],
                in_=out_rows[b][:, i * L : (i + 1) * L],
            )

        for t in range(PACK):
            regroup_w(t, "scalar" if t == PACK - 1 else "vector")
        quantise(w_mx, 0, D // 2)
        quantise(w_mx, D // 2, D)
        transpose_x(0)
        transpose_x(1)
        regroup_x(0, 0, "scalar")
        regroup_x(0, 1, "scalar")
        quantise_x(0)
        regroup_x(1, 0, "scalar")
        regroup_x(1, 1, "vector")
        quantise_x(1)
        first_matmul(0)
        transpose_x(2)

        steps = 2 * B
        for j in range(steps + 1):
            last_step = j == steps - 1
            if j < steps:
                tile_a, tile_b = tiles_of(j)
                round_h(tile_a, "scalar")
                round_h(tile_b, "vector" if last_step else "scalar")
                quantise_h(tile_a)
                if last_step:
                    quantise_h(tile_b)
            if j > 0:
                ready_a, ready_b = tiles_of(j - 1)
                store_sim(ready_a, "scalar")
                store_sim(ready_b, "vector")
            if j < steps - 1:
                quantise_h(tile_b)
            if j + 2 < 2 * B:
                regroup_x(j + 2, 0, "scalar")
                regroup_x(j + 2, 1, "vector")
                quantise_x(j + 2)
            if j + 1 < steps:
                first_matmul(j + 1)
            if j < steps:
                second_matmul(j)
            if j + 3 < 2 * B:
                transpose_x(j + 3)
